import numpy as np
import ml_dtypes


def mxq(x, axis, fmt="e4m3"):
    dtype, down = {"e4m3": (ml_dtypes.float8_e4m3fn, 7), "e5m2": (ml_dtypes.float8_e5m2, 14)}[fmt]
    v = np.moveaxis(np.asarray(x, np.float32).astype(ml_dtypes.bfloat16).astype(np.float64), axis, -1)
    blocks = v.reshape(v.shape[:-1] + (-1, 32))
    amax = np.abs(blocks).max(-1, keepdims=True)
    byte = np.maximum(np.where(amax > 0, np.frexp(amax)[1] - 1 + 127, 0) - down, 1)
    scale = np.exp2(byte - 127.0)
    codes = (blocks / scale).astype(np.float32).astype(dtype).astype(np.float64)
    return np.moveaxis((codes * scale).reshape(v.shape), -1, axis)


WIDE = False


def mx_kscale(k):
    if not WIDE:
        return np.ones(k)
    levels = np.array([10, -10, 5, -5, 0])
    a = np.random.permutation(np.resize(levels, k // 512 * 4)).reshape(k // 512, 4)
    idx = np.arange(k)
    return np.exp2(a[idx // 512, idx % 128 // 32])


BF16 = ml_dtypes.bfloat16


def bf(x):
    return np.asarray(x, np.float32).astype(BF16)


def f64(x):
    return np.asarray(x).astype(np.float64)


E2M1 = np.array([0.0, 0.5, 1.0, 1.5, 2.0, 3.0, 4.0, 6.0, -0.0, -0.5, -1.0, -1.5, -2.0, -3.0, -4.0, -6.0])


def pack_weight(w, fmt):
    k, n = w.shape
    w = f64(bf(w)).reshape(k // 32, 32, n)
    amax = np.abs(w).max(1)
    if fmt == "e4m3":
        byte = np.frexp(amax)[1] - 1 + 127 - 7
    else:
        mant, ex = np.frexp(amax / 6.0)
        byte = np.where(mant > 0.5, ex, ex - 1) + 127
    byte = np.clip(np.where(amax > 0, byte, 1), 1, 254)
    scaled = (w * np.exp2(127.0 - byte)[:, None, :]).reshape(k, n).astype(np.float32)
    by_word = np.ascontiguousarray(scaled.reshape(k // 512, 128, 4, n).transpose(0, 1, 3, 2))
    if fmt == "e4m3":
        words = by_word.astype(ml_dtypes.float8_e4m3fn).view(np.uint8)
    else:
        c = by_word.astype(ml_dtypes.float4_e2m1fn).view(np.uint8) & 0xF
        words = c[..., 0::2] | (c[..., 1::2] << 4)
    return np.ascontiguousarray(words), np.ascontiguousarray(byte.astype(np.uint8).reshape(k // 512, 16, n))


def unpack_weight(words, scales, fmt):
    g, p, n, _ = words.shape
    if fmt == "e4m3":
        vals = np.ascontiguousarray(words).view(ml_dtypes.float8_e4m3fn).astype(np.float64)
    else:
        nib = np.empty((g, p, n, 4), np.uint8)
        nib[..., 0::2] = words & 0xF
        nib[..., 1::2] = words >> 4
        vals = E2M1[nib]
    vals = vals * np.repeat(np.exp2(scales.astype(np.float64) - 127.0), 8, axis=1)[..., None]
    return vals.transpose(0, 1, 3, 2).reshape(g * 512, n)


B, D_IN, D_HID, D_OUT = 1024, 512, 4096, 512
EPS = 1e-12
NORM_MAX = 16
FMT = "e4m3"


def setup_inputs():
    s, t = mx_kscale(D_IN), mx_kscale(D_HID)
    x = bf(np.random.standard_normal((B, D_IN)))
    in_mean = bf(np.random.standard_normal(D_IN) * 0.1)
    in_std = bf(np.random.uniform(0.5, 1.5, D_IN) / s)
    out_mean = bf(np.random.standard_normal(D_OUT) * 0.1)
    out_std = bf(np.random.uniform(0.5, 1.5, D_OUT))
    W1 = np.random.standard_normal((D_HID, D_IN)) / np.sqrt(D_IN) / s[None, :] * t[:, None]
    b1 = bf(np.random.standard_normal(D_HID) * 0.1 * t)
    W2 = np.random.standard_normal((D_OUT, D_HID)) * 0.85 / np.sqrt(D_HID) / t[None, :]
    b2 = bf(np.random.standard_normal(D_OUT) * 0.1)
    W1_words, W1_scales = pack_weight(np.ascontiguousarray(W1.T), FMT)
    W2_words, W2_scales = pack_weight(np.ascontiguousarray(W2.T), FMT)
    return {
        "x": x,
        "in_mean": in_mean,
        "in_std": in_std,
        "out_mean": out_mean,
        "out_std": out_std,
        "W1_words": W1_words,
        "W1_scales": W1_scales,
        "b1": b1,
        "W2_words": W2_words,
        "W2_scales": W2_scales,
        "b2": b2,
        "norm_max": NORM_MAX,
    }


def reference(x, in_mean, in_std, out_mean, out_std, W1_words, W1_scales, b1, W2_words, W2_scales, b2, norm_max):
    x, in_mean, in_std, out_mean, out_std = f64(x), f64(in_mean), f64(in_std), f64(out_mean), f64(out_std)
    norm_max = float(norm_max)
    x_copy = x[..., :D_OUT]
    xn = (x - in_mean) / in_std
    h = np.maximum((mxq(xn, 1, "e4m3") @ unpack_weight(W1_words, W1_scales, FMT)) + f64(b1), 0.0)
    res = (mxq(h, 1, "e4m3") @ unpack_weight(W2_words, W2_scales, FMT)) + f64(b2)
    norms = np.sqrt((res * res).sum(-1, keepdims=True))
    scale = norm_max / norms
    res = np.where(norms > norm_max, res * scale, res)
    res = res * out_std + out_mean - in_mean
    mapped = res + x_copy
    mnorm = np.sqrt((mapped * mapped).sum(-1, keepdims=True))
    return mapped / np.maximum(mnorm, EPS)

@@ -1,0 +1,273 @@
+from contextlib import ExitStack
+
+import concourse.mybir as mybir
+from concourse.masks import make_identity
+
+F32 = mybir.dt.float32
+BF16 = mybir.dt.bfloat16
+I32 = mybir.dt.int32
+U32 = mybir.dt.uint32
+U8 = mybir.dt.uint8
+FP8X4 = mybir.dt.float8_e4m3fn_x4
+ALU = mybir.AluOpType
+ACT = mybir.ActivationFunctionType
+
+P = 128
+PACK = 4
+K_PASS = P * PACK
+BATCH, D_IN, D_HID, D_OUT = 1024, 512, 4096, 512
+N_TILES = BATCH // P
+N_GROUPS = D_HID // K_PASS
+HALF = N_GROUPS // 2
+N_STEPS = 2 * N_TILES
+EPS = 1e-12
+
+FLOPS = 2 * BATCH * D_IN * D_HID + 2 * BATCH * D_HID * D_OUT
+
+
+def tile_mlp_kernel(
+    tc, x, in_mean, in_std, out_mean, out_std, W1_words, W1_scales, b1, W2_words, W2_scales, b2, norm_max, out
+):
+    nc = tc.nc
+    with ExitStack() as ctx:
+        ctx.enter_context(tc.manual_schedule())
+        keep = ctx.enter_context(tc.tile_pool(name="keep", bufs=1))
+        xwork = ctx.enter_context(tc.tile_pool(name="xwork", bufs=3))
+        hwork = ctx.enter_context(tc.tile_pool(name="hwork", bufs=3))
+        codes = ctx.enter_context(tc.tile_pool(name="codes", bufs=4))
+        tail = ctx.enter_context(tc.tile_pool(name="tail", bufs=3))
+        small = ctx.enter_context(tc.tile_pool(name="small", bufs=4))
+        hp_pool = ctx.enter_context(tc.psum_pool(name="hp_pool", bufs=4))
+        tp_pool = ctx.enter_context(tc.psum_pool(name="tp_pool", bufs=2))
+        acc_pool = ctx.enter_context(tc.psum_pool(name="acc_pool", bufs=2))
+
+        mean_bc = keep.tile([P, D_IN], BF16)
+        std_bc = keep.tile([P, D_IN], BF16)
+        x_sb = keep.tile([P, N_TILES, D_IN], BF16)
+        b1_bc = keep.tile([P, D_HID], BF16)
+        omean_bc = keep.tile([P, D_OUT], BF16)
+        ostd_bc = keep.tile([P, D_OUT], BF16)
+        b2_bc = keep.tile([P, D_OUT], BF16)
+        x_rows = x.rearrange("(n p) k -> p n k", p=P)
+        nc.scalar.dma_start(out=mean_bc[:], in_=in_mean.partition_broadcast(P))
+        nc.scalar.dma_start(out=std_bc[:], in_=in_std.partition_broadcast(P))
+        nc.scalar.dma_start(out=x_sb[:, 0:2, :], in_=x_rows[:, 0:2, :])
+        nc.scalar.dma_start(out=b1_bc[:], in_=b1.partition_broadcast(P))
+        nc.scalar.dma_start(out=x_sb[:, 2:N_TILES, :], in_=x_rows[:, 2:N_TILES, :])
+        nc.scalar.dma_start(out=omean_bc[:], in_=out_mean.partition_broadcast(P))
+        nc.scalar.dma_start(out=ostd_bc[:], in_=out_std.partition_broadcast(P))
+        nc.scalar.dma_start(out=b2_bc[:], in_=b2.partition_broadcast(P))
+
+        w1_words = keep.tile([P, D_HID * PACK], U8, align_bytes=64)
+        w1_planes = keep.tile([P, D_HID], U8, align_bytes=64)
+        w2_words = keep.tile([P, N_GROUPS, D_OUT * PACK], U8, align_bytes=64)
+        w2_planes = keep.tile([P, N_GROUPS, D_OUT], U8, align_bytes=64)
+        nc.vector.memset(w1_planes[:].bitcast(I32), 0)
+        nc.vector.memset(w2_planes[:].bitcast(I32), 0)
+        for q in range(4):
+            nc.sync.dma_start(
+                out=w1_planes[32 * q : 32 * q + 4, :].bitcast(I32),
+                in_=W1_scales[0, 4 * q : 4 * q + 4, :].bitcast(I32),
+            )
+        w1_dram = W1_words[0].rearrange("p n t -> p (n t)")
+        chunk = K_PASS * PACK
+        for a in range(N_GROUPS // 2):
+            nc.sync.dma_start(
+                out=w1_words[:, 2 * a * chunk : (2 * a + 2) * chunk].bitcast(I32),
+                in_=w1_dram[:, 2 * a * chunk : (2 * a + 2) * chunk].bitcast(I32),
+            )
+        for q in range(4):
+            nc.sync.dma_start(
+                out=w2_planes[32 * q : 32 * q + 4, :, :].bitcast(I32),
+                in_=W2_scales[:, 4 * q : 4 * q + 4, :].rearrange("g r n -> r g n").bitcast(I32),
+            )
+        w2_dram = W2_words.rearrange("g p n t -> p g (n t)")
+        for a in range(N_GROUPS // 2):
+            nc.sync.dma_start(
+                out=w2_words[:, 2 * a : 2 * a + 2, :].bitcast(I32),
+                in_=w2_dram[:, 2 * a : 2 * a + 2, :].bitcast(I32),
+            )
+
+        ident = keep.tile([P, P], F32)
+        make_identity(nc, ident[:])
+        warm = keep.tile([P, 1], F32)
+        nc.vector.memset(warm[:], 1.0)
+        nc.scalar.activation(out=warm[:], in_=warm[:], func=ACT.Abs_reciprocal_sqrt)
+        rstd_bc = keep.tile([P, D_IN], F32)
+        nc.vector.reciprocal(out=rstd_bc[:], in_=std_bc[:])
+        resid = keep.tile([P, N_TILES, D_OUT], F32)
+
+        xn_tiles = {}
+        x_codes = {}
+        h_sorted = {}
+        h_grouped = {}
+        h_codes = {}
+        accs = {}
+        parts = {}
+
+        def normalise_x(i):
+            diff = xwork.tile([P, D_IN], F32)
+            nc.gpsimd.tensor_tensor(out=diff[:], in0=x_sb[:, i, :], in1=mean_bc[:], op=ALU.subtract)
+            xn = xwork.tile([P, 2, 2 * P], BF16)
+            nc.gpsimd.tensor_tensor(
+                out=xn[:].rearrange("b u (p e) -> b u p e", e=2),
+                in0=diff[:].rearrange("b (p u e) -> b u p e", u=2, e=2),
+                in1=rstd_bc[:].rearrange("b (p u e) -> b u p e", u=2, e=2),
+                op=ALU.mult,
+            )
+            nc.gpsimd.tensor_tensor(out=resid[:, i, :], in0=diff[:], in1=omean_bc[:], op=ALU.add)
+            xn_tiles[i] = xn
+
+        def turn_x(i):
+            xn = xn_tiles[i]
+            xt = tp_pool.tile([P, 2, P], F32, tag="tp")
+            for u in range(2):
+                nc.tensor.transpose(xt[:, u, :], xn[:, u, :].bitcast(F32), ident[:])
+            xg = xwork.tile([P, P * PACK], BF16, align_bytes=64)
+            nc.scalar.copy(
+                out=xg[:].rearrange("p (b u e) -> p b u e", u=2, e=2),
+                in_=xt[:].bitcast(BF16).rearrange("p u (b e) -> p b u e", e=2),
+            )
+            return xg
+
+        def quantise_x(i, xg):
+            xq = codes.tile([P, P], U32, align_bytes=64)
+            xs = codes.tile([P, P], U8, align_bytes=64)
+            nc.vector.quantize_mx(out=xq[:].bitcast(FP8X4), scales=xs[:], in_=xg[:])
+            x_codes[i] = (xq, xs)
+
+        def layer1(s):
+            i, half = divmod(s, 2)
+            xq, xs = x_codes[i]
+            hs = hwork.tile([P, HALF, 2, 2 * P], BF16)
+            for j in range(HALF):
+                g = half * HALF + j
+                hp = hp_pool.tile([P, K_PASS], F32)
+                nc.tensor.matmul_mx(
+                    out=hp[:],
+                    lhsT=xq[:].bitcast(FP8X4),
+                    lhsT_scale=xs[:],
+                    rhs=w1_words[:, g * chunk : (g + 1) * chunk].bitcast(FP8X4),
+                    rhs_scale=w1_planes[:, g * K_PASS : (g + 1) * K_PASS],
+                    start=True,
+                    stop=True,
+                )
+                nc.vector.tensor_tensor(
+                    out=hs[:, j, :, :].rearrange("b u (p e) -> b u p e", e=2),
+                    in0=hp[:].rearrange("b (p u e) -> b u p e", u=2, e=2),
+                    in1=b1_bc[:, g * K_PASS : (g + 1) * K_PASS].rearrange("b (p u e) -> b u p e", u=2, e=2),
+                    op=ALU.add,
+                )
+            h_sorted[s] = hs
+
+        def turn_h(s):
+            hs = h_sorted[s]
+            hg = hwork.tile([P, HALF * P * PACK], BF16, align_bytes=64)
+            width = 2 * P * PACK
+            for pair in range(HALF // 2):
+                tp = tp_pool.tile([P, 2, 2 * P], F32, tag="tp")
+                for gi in range(2):
+                    for u in range(2):
+                        nc.tensor.transpose(
+                            tp[:, u, gi * P : (gi + 1) * P], hs[:, 2 * pair + gi, u, :].bitcast(F32), ident[:]
+                        )
+                nc.scalar.activation(
+                    out=hg[:, pair * width : (pair + 1) * width].rearrange("p (m u e) -> p m u e", u=2, e=2),
+                    in_=tp[:].bitcast(BF16).rearrange("p u (m e) -> p m u e", e=2),
+                    func=ACT.Relu,
+                )
+            h_grouped[s] = hg
+
+        def quantise_h(s):
+            hq = codes.tile([P, HALF * P], U32, align_bytes=64)
+            hsc = codes.tile([P, HALF * P], U8, align_bytes=64)
+            nc.vector.quantize_mx(out=hq[:].bitcast(FP8X4), scales=hsc[:], in_=h_grouped[s][:])
+            h_codes[s] = (hq, hsc)
+
+        def layer2(s):
+            i, half = divmod(s, 2)
+            if half == 0:
+                acc_new = acc_pool.tile([P, D_OUT], F32, name="acc")
+                accs[i] = acc_new
+            acc = accs[i]
+            hq, hsc = h_codes[s]
+            for j in range(HALF):
+                g = half * HALF + j
+                nc.tensor.matmul_mx(
+                    out=acc[:],
+                    lhsT=hq[:, j * P : (j + 1) * P].bitcast(FP8X4),
+                    lhsT_scale=hsc[:, j * P : (j + 1) * P],
+                    rhs=w2_words[:, g, :].bitcast(FP8X4),
+                    rhs_scale=w2_planes[:, g, :],
+                    start=(g == 0),
+                    stop=(g == N_GROUPS - 1),
+                )
+
+        limit_sq = float(norm_max) * float(norm_max)
+        out_tiles = out.rearrange("(n p) o -> n p o", p=P)
+
+        def finish_a(i):
+            res = tail.tile([P, D_OUT], F32)
+            nc.vector.tensor_tensor(out=res[:], in0=accs[i][:], in1=b2_bc[:], op=ALU.add)
+            wide = tail.tile([P, D_OUT], F32)
+            nc.gpsimd.tensor_tensor(out=wide[:], in0=res[:], in1=ostd_bc[:], op=ALU.mult)
+            parts[i] = (res, wide)
+
+        def finish_b(i):
+            res, wide = parts[i]
+            junk = tail.tile([P, D_OUT], BF16)
+            ss1 = small.tile([P, 1], F32)
+            nc.scalar.activation(out=junk[:], in_=res[:], func=ACT.Square, accum_out=ss1[:])
+            over = small.tile([P, 1], F32)
+            nc.scalar.activation(out=over[:], in_=ss1[:], func=ACT.Relu, scale=1.0 / limit_sq, bias=-1.0)
+            clamp = small.tile([P, 1], F32)
+            nc.scalar.activation(out=clamp[:], in_=over[:], func=ACT.Abs_reciprocal_sqrt, bias=1.0)
+            mapped = tail.tile([P, D_OUT], F32)
+            nc.vector.scalar_tensor_tensor(
+                out=mapped[:], in0=wide[:], scalar=clamp[:], in1=resid[:, i, :], op0=ALU.mult, op1=ALU.add
+            )
+            parts[i] = mapped
+
+        def finish_c(i):
+            mapped = parts[i]
+            junk = tail.tile([P, D_OUT], BF16)
+            ss2 = small.tile([P, 1], F32)
+            nc.scalar.activation(out=junk[:], in_=mapped[:], func=ACT.Square, accum_out=ss2[:])
+            over2 = small.tile([P, 1], F32)
+            nc.scalar.activation(out=over2[:], in_=ss2[:], func=ACT.Relu, bias=-EPS * EPS)
+            rnorm = small.tile([P, 1], F32)
+            nc.scalar.activation(out=rnorm[:], in_=over2[:], func=ACT.Abs_reciprocal_sqrt, bias=EPS * EPS)
+            result = tail.tile([P, D_OUT], F32)
+            nc.gpsimd.tensor_scalar(
+                out=result[:], in0=mapped[:], scalar1=rnorm[:], scalar2=0.0, op0=ALU.mult, op1=ALU.add
+            )
+            nc.sync.dma_start(out=out_tiles[i], in_=result[:])
+
+        for i in range(3):
+            normalise_x(i)
+        for i in range(2):
+            quantise_x(i, turn_x(i))
+        layer1(0)
+        for s in range(N_STEPS + 4):
+            i, half = divmod(s, 2)
+            if s + 1 < N_STEPS:
+                layer1(s + 1)
+            if half == 0 and i + 3 < N_TILES:
+                normalise_x(i + 3)
+            xg = None
+            if half == 1 and i + 2 < N_TILES:
+                xg = turn_x(i + 2)
+            if s < N_STEPS:
+                turn_h(s)
+            if xg is not None:
+                quantise_x(i + 2, xg)
+            if s < N_STEPS:
+                quantise_h(s)
+            if 1 <= s <= N_STEPS:
+                layer2(s - 1)
+            if half == 0 and 1 <= i <= N_TILES:
+                finish_a(i - 1)
+            if half == 1 and 1 <= i <= N_TILES:
+                finish_b(i - 1)
+            if half == 0 and 2 <= i <= N_TILES + 1:
+                finish_c(i - 2)

@@ -18,8 +18,10 @@ K_PASS = P * PACK
 BATCH, D_IN, D_HID, D_OUT = 1024, 512, 4096, 512
 N_TILES = BATCH // P
 N_GROUPS = D_HID // K_PASS
-HALF = N_GROUPS // 2
-N_STEPS = 2 * N_TILES
+PAIR = 2
+WIDTH = PAIR * P
+N_PAIRS = N_TILES // PAIR
+N_UNITS = N_PAIRS * N_GROUPS
 EPS = 1e-12
 
 FLOPS = 2 * BATCH * D_IN * D_HID + 2 * BATCH * D_HID * D_OUT
@@ -32,242 +34,361 @@ def tile_mlp_kernel(
     with ExitStack() as ctx:
         ctx.enter_context(tc.manual_schedule())
         keep = ctx.enter_context(tc.tile_pool(name="keep", bufs=1))
-        xwork = ctx.enter_context(tc.tile_pool(name="xwork", bufs=3))
-        hwork = ctx.enter_context(tc.tile_pool(name="hwork", bufs=3))
+        rows = ctx.enter_context(tc.tile_pool(name="rows", bufs=3))
+        grouped = ctx.enter_context(tc.tile_pool(name="grouped", bufs=3))
         codes = ctx.enter_context(tc.tile_pool(name="codes", bufs=4))
-        tail = ctx.enter_context(tc.tile_pool(name="tail", bufs=3))
+        tail = ctx.enter_context(tc.tile_pool(name="tail", bufs=4))
         small = ctx.enter_context(tc.tile_pool(name="small", bufs=4))
         hp_pool = ctx.enter_context(tc.psum_pool(name="hp_pool", bufs=4))
-        tp_pool = ctx.enter_context(tc.psum_pool(name="tp_pool", bufs=2))
-        acc_pool = ctx.enter_context(tc.psum_pool(name="acc_pool", bufs=2))
+        acc_pool = ctx.enter_context(tc.psum_pool(name="acc_pool", bufs=4))
 
-        mean_bc = keep.tile([P, D_IN], BF16)
-        std_bc = keep.tile([P, D_IN], BF16)
         x_sb = keep.tile([P, N_TILES, D_IN], BF16)
-        b1_bc = keep.tile([P, D_HID], BF16)
-        omean_bc = keep.tile([P, D_OUT], BF16)
-        ostd_bc = keep.tile([P, D_OUT], BF16)
-        b2_bc = keep.tile([P, D_OUT], BF16)
-        x_rows = x.rearrange("(n p) k -> p n k", p=P)
-        nc.scalar.dma_start(out=mean_bc[:], in_=in_mean.partition_broadcast(P))
-        nc.scalar.dma_start(out=std_bc[:], in_=in_std.partition_broadcast(P))
-        nc.scalar.dma_start(out=x_sb[:, 0:2, :], in_=x_rows[:, 0:2, :])
-        nc.scalar.dma_start(out=b1_bc[:], in_=b1.partition_broadcast(P))
-        nc.scalar.dma_start(out=x_sb[:, 2:N_TILES, :], in_=x_rows[:, 2:N_TILES, :])
-        nc.scalar.dma_start(out=omean_bc[:], in_=out_mean.partition_broadcast(P))
-        nc.scalar.dma_start(out=ostd_bc[:], in_=out_std.partition_broadcast(P))
-        nc.scalar.dma_start(out=b2_bc[:], in_=b2.partition_broadcast(P))
-
-        w1_words = keep.tile([P, D_HID * PACK], U8, align_bytes=64)
-        w1_planes = keep.tile([P, D_HID], U8, align_bytes=64)
+        mean4 = keep.tile([P, PACK], BF16)
+        std4 = keep.tile([P, PACK], BF16)
+        b1_raw = keep.tile([P, N_GROUPS, PACK], BF16)
+        vec_rows = keep.tile([P, D_OUT], BF16)
+        w1_raw = keep.tile([P, D_HID], I32)
+        w1_words = keep.tile([P, N_GROUPS, PACK, P], I32, align_bytes=64)
+        w1s_raw = keep.tile([P, D_HID], U8)
+        w1_planes = keep.tile([P, N_GROUPS, PACK, P], U8, align_bytes=64)
         w2_words = keep.tile([P, N_GROUPS, D_OUT * PACK], U8, align_bytes=64)
         w2_planes = keep.tile([P, N_GROUPS, D_OUT], U8, align_bytes=64)
-        nc.vector.memset(w1_planes[:].bitcast(I32), 0)
+        x_words = keep.tile([P, BATCH], U32, align_bytes=64)
+        x_planes = keep.tile([P, BATCH], U8, align_bytes=64)
+
+        nc.vector.memset(w1s_raw[:].bitcast(I32), 0)
+        nc.vector.memset(vec_rows[:], 0.0)
         nc.vector.memset(w2_planes[:].bitcast(I32), 0)
+        warm = keep.tile([P, 1], F32)
+        nc.vector.memset(warm[:], 1.0)
+        nc.scalar.activation(out=warm[:], in_=warm[:], func=ACT.Abs_reciprocal_sqrt)
+        ident = keep.tile([P, P], F32)
+        make_identity(nc, ident[:])
+        ident_bf = keep.tile([P, P], BF16)
+        make_identity(nc, ident_bf[:])
+
+        x_rows = x.rearrange("(n p) k -> p n k", p=P)
+        w1_dram = W1_words[0].rearrange("p n t -> p (n t)")
+        w2_dram = W2_words.rearrange("g p n t -> p g (n t)")
+        chunk = K_PASS * PACK
+
+        def load_x(j):
+            nc.sync.dma_start(out=x_sb[:, PAIR * j : PAIR * (j + 1), :], in_=x_rows[:, PAIR * j : PAIR * (j + 1), :])
+
+        def load_w1(g):
+            nc.sync.dma_start(
+                out=w1_raw[:, g * K_PASS : (g + 1) * K_PASS], in_=w1_dram[:, g * chunk : (g + 1) * chunk].bitcast(I32)
+            )
+
+        def load_w2(g):
+            nc.sync.dma_start(out=w2_words[:, g : g + 1, :].bitcast(I32), in_=w2_dram[:, g : g + 1, :].bitcast(I32))
+
+        nc.sync.dma_start(out=mean4[:], in_=in_mean.rearrange("(p t) -> p t", t=PACK))
+        nc.sync.dma_start(out=std4[:], in_=in_std.rearrange("(p t) -> p t", t=PACK))
+        load_x(0)
         for q in range(4):
             nc.sync.dma_start(
-                out=w1_planes[32 * q : 32 * q + 4, :].bitcast(I32),
+                out=w1s_raw[32 * q : 32 * q + 4, :].bitcast(I32),
                 in_=W1_scales[0, 4 * q : 4 * q + 4, :].bitcast(I32),
             )
-        w1_dram = W1_words[0].rearrange("p n t -> p (n t)")
-        chunk = K_PASS * PACK
-        for a in range(N_GROUPS // 2):
-            nc.sync.dma_start(
-                out=w1_words[:, 2 * a * chunk : (2 * a + 2) * chunk].bitcast(I32),
-                in_=w1_dram[:, 2 * a * chunk : (2 * a + 2) * chunk].bitcast(I32),
-            )
+        load_w1(0)
+        nc.sync.dma_start(out=b1_raw[:], in_=b1.rearrange("(g p t) -> p g t", p=P, t=PACK))
+        load_x(1)
+        for r, vec in enumerate((out_mean, in_mean, b2, out_std)):
+            nc.sync.dma_start(out=vec_rows[r : r + 1, :], in_=vec.rearrange("(o n) -> o n", o=1))
+        for g in range(1, 5):
+            load_w1(g)
         for q in range(4):
             nc.sync.dma_start(
                 out=w2_planes[32 * q : 32 * q + 4, :, :].bitcast(I32),
                 in_=W2_scales[:, 4 * q : 4 * q + 4, :].rearrange("g r n -> r g n").bitcast(I32),
             )
-        w2_dram = W2_words.rearrange("g p n t -> p g (n t)")
-        for a in range(N_GROUPS // 2):
-            nc.sync.dma_start(
-                out=w2_words[:, 2 * a : 2 * a + 2, :].bitcast(I32),
-                in_=w2_dram[:, 2 * a : 2 * a + 2, :].bitcast(I32),
-            )
+        load_w2(0)
+        load_w1(5)
+        load_w2(1)
+        load_w1(6)
+        load_w2(2)
+        load_w1(7)
+        for g in range(3, N_GROUPS):
+            load_w2(g)
+        load_x(2)
+        load_x(3)
 
-        ident = keep.tile([P, P], F32)
-        make_identity(nc, ident[:])
-        warm = keep.tile([P, 1], F32)
-        nc.vector.memset(warm[:], 1.0)
-        nc.scalar.activation(out=warm[:], in_=warm[:], func=ACT.Abs_reciprocal_sqrt)
-        rstd_bc = keep.tile([P, D_IN], F32)
-        nc.vector.reciprocal(out=rstd_bc[:], in_=std_bc[:])
+        rstd4 = keep.tile([P, PACK], F32)
+        nc.vector.reciprocal(out=rstd4[:], in_=std4[:])
+        shift4 = keep.tile([P, PACK], F32)
+        nc.vector.scalar_tensor_tensor(
+            out=shift4[:], in0=mean4[:], scalar=-1.0, in1=rstd4[:], op0=ALU.mult, op1=ALU.mult
+        )
+        sign_col = keep.tile([P, 1], BF16)
+        nc.vector.tensor_tensor(out=sign_col[:], in0=ident_bf[:, 0:1], in1=ident_bf[:, 1:2], op=ALU.subtract)
+        b1_cols = keep.tile([P, N_GROUPS * PACK], F32)
+        shift_bc = keep.tile([P, D_OUT], F32)
+        b2_bc = keep.tile([P, D_OUT], F32)
+        ostd_bc = keep.tile([P, D_OUT], F32)
         resid = keep.tile([P, N_TILES, D_OUT], F32)
 
-        xn_tiles = {}
-        x_codes = {}
-        h_sorted = {}
-        h_grouped = {}
+        banks = {}
+        row_tiles = {}
+        grouped_tiles = {}
         h_codes = {}
         accs = {}
         parts = {}
 
-        def normalise_x(i):
-            diff = xwork.tile([P, D_IN], F32)
-            nc.gpsimd.tensor_tensor(out=diff[:], in0=x_sb[:, i, :], in1=mean_bc[:], op=ALU.subtract)
-            xn = xwork.tile([P, 2, 2 * P], BF16)
-            nc.gpsimd.tensor_tensor(
-                out=xn[:].rearrange("b u (p e) -> b u p e", e=2),
-                in0=diff[:].rearrange("b (p u e) -> b u p e", u=2, e=2),
-                in1=rstd_bc[:].rearrange("b (p u e) -> b u p e", u=2, e=2),
-                op=ALU.mult,
+        def permute_w1(g):
+            nc.vector.tensor_copy(
+                out=w1_words[:, g, :, :],
+                in_=w1_raw[:, g * K_PASS : (g + 1) * K_PASS].rearrange("p (m t) -> p t m", t=PACK),
             )
-            nc.gpsimd.tensor_tensor(out=resid[:, i, :], in0=diff[:], in1=omean_bc[:], op=ALU.add)
-            xn_tiles[i] = xn
-
-        def turn_x(i):
-            xn = xn_tiles[i]
-            xt = tp_pool.tile([P, 2, P], F32, tag="tp")
-            for u in range(2):
-                nc.tensor.transpose(xt[:, u, :], xn[:, u, :].bitcast(F32), ident[:])
-            xg = xwork.tile([P, P * PACK], BF16, align_bytes=64)
-            nc.scalar.copy(
-                out=xg[:].rearrange("p (b u e) -> p b u e", u=2, e=2),
-                in_=xt[:].bitcast(BF16).rearrange("p u (b e) -> p b u e", e=2),
+            nc.vector.tensor_copy(
+                out=w1_planes[:, g, :, :],
+                in_=w1s_raw[:, g * K_PASS : (g + 1) * K_PASS].rearrange("p (m t) -> p t m", t=PACK),
             )
-            return xg
 
-        def quantise_x(i, xg):
-            xq = codes.tile([P, P], U32, align_bytes=64)
-            xs = codes.tile([P, P], U8, align_bytes=64)
-            nc.vector.quantize_mx(out=xq[:].bitcast(FP8X4), scales=xs[:], in_=xg[:])
-            x_codes[i] = (xq, xs)
+        def turn_x(j):
+            xt = hp_pool.tile([P, PAIR, 2, P], F32, tag="hp")
+            for i in range(PAIR):
+                words = x_sb[:, PAIR * j + i, :].bitcast(F32).rearrange("b (p u) -> b u p", u=2)
+                for u in range(2):
+                    nc.tensor.transpose(xt[:, i, u, :], words[:, u, :], ident[:])
+            banks["x", j] = xt
 
-        def layer1(s):
-            i, half = divmod(s, 2)
-            xq, xs = x_codes[i]
-            hs = hwork.tile([P, HALF, 2, 2 * P], BF16)
-            for j in range(HALF):
-                g = half * HALF + j
-                hp = hp_pool.tile([P, K_PASS], F32)
+        def normalise_x(j, t_list):
+            if ("x", j) not in row_tiles:
+                x_new = rows.tile([P, PACK, WIDTH], BF16, tag="rows")
+                row_tiles["x", j] = x_new
+            xr = row_tiles["x", j]
+            view = banks["x", j][:].rearrange("p i u b -> p (i u b)").bitcast(BF16)
+            view = view.rearrange("p (i u b e) -> p u e i b", i=PAIR, u=2, e=2)
+            for t in t_list:
+                nc.scalar.activation(
+                    out=xr[:, t, :].rearrange("p (i b) -> p i b", i=PAIR),
+                    in_=view[:, t // 2, t % 2, :, :],
+                    func=ACT.Identity,
+                    scale=rstd4[:, t : t + 1],
+                    bias=shift4[:, t : t + 1],
+                )
+
+        def interleave(key):
+            g_new = grouped.tile([P, WIDTH * PACK], BF16, align_bytes=64, tag="grouped")
+            nc.vector.tensor_copy(
+                out=g_new[:].rearrange("p (c t) -> p c t", t=PACK), in_=row_tiles[key][:].rearrange("p t c -> p c t")
+            )
+            grouped_tiles[key] = g_new
+
+        def quantise_x(j):
+            cols = slice(j * WIDTH, (j + 1) * WIDTH)
+            nc.vector.quantize_mx(
+                out=x_words[:, cols].bitcast(FP8X4), scales=x_planes[:, cols], in_=grouped_tiles["x", j][:]
+            )
+
+        def layer1_half(s, half):
+            j, g = divmod(s, N_GROUPS)
+            cols = slice(j * WIDTH, (j + 1) * WIDTH)
+            hp = hp_pool.tile([P, 2, WIDTH], F32, tag="hp")
+            for e in range(2):
+                t = 2 * half + e
                 nc.tensor.matmul_mx(
-                    out=hp[:],
-                    lhsT=xq[:].bitcast(FP8X4),
-                    lhsT_scale=xs[:],
-                    rhs=w1_words[:, g * chunk : (g + 1) * chunk].bitcast(FP8X4),
-                    rhs_scale=w1_planes[:, g * K_PASS : (g + 1) * K_PASS],
+                    out=hp[:, e, :],
+                    lhsT=w1_words[:, g, t, :].bitcast(FP8X4),
+                    lhsT_scale=w1_planes[:, g, t, :],
+                    rhs=x_words[:, cols].bitcast(FP8X4),
+                    rhs_scale=x_planes[:, cols],
                     start=True,
                     stop=True,
                 )
-                nc.vector.tensor_tensor(
-                    out=hs[:, j, :, :].rearrange("b u (p e) -> b u p e", e=2),
-                    in0=hp[:].rearrange("b (p u e) -> b u p e", u=2, e=2),
-                    in1=b1_bc[:, g * K_PASS : (g + 1) * K_PASS].rearrange("b (p u e) -> b u p e", u=2, e=2),
-                    op=ALU.add,
-                )
-            h_sorted[s] = hs
+            banks[s, half] = hp
 
-        def turn_h(s):
-            hs = h_sorted[s]
-            hg = hwork.tile([P, HALF * P * PACK], BF16, align_bytes=64)
-            width = 2 * P * PACK
-            for pair in range(HALF // 2):
-                tp = tp_pool.tile([P, 2, 2 * P], F32, tag="tp")
-                for gi in range(2):
-                    for u in range(2):
-                        nc.tensor.transpose(
-                            tp[:, u, gi * P : (gi + 1) * P], hs[:, 2 * pair + gi, u, :].bitcast(F32), ident[:]
-                        )
+        def bias_relu(s):
+            g = s % N_GROUPS
+            hr = rows.tile([P, PACK, WIDTH], BF16, tag="rows")
+            for t in range(PACK):
                 nc.scalar.activation(
-                    out=hg[:, pair * width : (pair + 1) * width].rearrange("p (m u e) -> p m u e", u=2, e=2),
-                    in_=tp[:].bitcast(BF16).rearrange("p u (m e) -> p m u e", e=2),
+                    out=hr[:, t, :],
+                    in_=banks[s, t // 2][:, t % 2, :],
                     func=ACT.Relu,
+                    bias=b1_cols[:, PACK * g + t : PACK * g + t + 1],
                 )
-            h_grouped[s] = hg
+            row_tiles[s] = hr
 
         def quantise_h(s):
-            hq = codes.tile([P, HALF * P], U32, align_bytes=64)
-            hsc = codes.tile([P, HALF * P], U8, align_bytes=64)
-            nc.vector.quantize_mx(out=hq[:].bitcast(FP8X4), scales=hsc[:], in_=h_grouped[s][:])
+            hq = codes.tile([P, WIDTH], U32, align_bytes=64)
+            hsc = codes.tile([P, WIDTH], U8, align_bytes=64)
+            nc.vector.quantize_mx(out=hq[:].bitcast(FP8X4), scales=hsc[:], in_=grouped_tiles[s][:])
             h_codes[s] = (hq, hsc)
 
-        def layer2(s):
-            i, half = divmod(s, 2)
-            if half == 0:
+        def layer2_tile(s, i):
+            j, g = divmod(s, N_GROUPS)
+            if g == 0:
                 acc_new = acc_pool.tile([P, D_OUT], F32, name="acc")
-                accs[i] = acc_new
-            acc = accs[i]
+                accs[PAIR * j + i] = acc_new
             hq, hsc = h_codes[s]
-            for j in range(HALF):
-                g = half * HALF + j
-                nc.tensor.matmul_mx(
-                    out=acc[:],
-                    lhsT=hq[:, j * P : (j + 1) * P].bitcast(FP8X4),
-                    lhsT_scale=hsc[:, j * P : (j + 1) * P],
-                    rhs=w2_words[:, g, :].bitcast(FP8X4),
-                    rhs_scale=w2_planes[:, g, :],
-                    start=(g == 0),
-                    stop=(g == N_GROUPS - 1),
-                )
+            nc.tensor.matmul_mx(
+                out=accs[PAIR * j + i][:],
+                lhsT=hq[:, i * P : (i + 1) * P].bitcast(FP8X4),
+                lhsT_scale=hsc[:, i * P : (i + 1) * P],
+                rhs=w2_words[:, g, :].bitcast(FP8X4),
+                rhs_scale=w2_planes[:, g, :],
+                start=(g == 0),
+                stop=(g == N_GROUPS - 1),
+            )
+
+        def spread(column, target):
+            ps = hp_pool.tile([P, D_OUT], F32, tag="hp")
+            nc.tensor.matmul(out=ps[:], lhsT=column.to_broadcast([P, P]), rhs=vec_rows[:], start=True, stop=True)
+            nc.scalar.copy(out=target[:], in_=ps[:])
+
+        def make_resid(i):
+            nc.vector.tensor_tensor(out=resid[:, i, :], in0=x_sb[:, i, :], in1=shift_bc[:], op=ALU.add)
 
         limit_sq = float(norm_max) * float(norm_max)
         out_tiles = out.rearrange("(n p) o -> n p o", p=P)
 
-        def finish_a(i):
+        def add_b2(i):
             res = tail.tile([P, D_OUT], F32)
             nc.vector.tensor_tensor(out=res[:], in0=accs[i][:], in1=b2_bc[:], op=ALU.add)
-            wide = tail.tile([P, D_OUT], F32)
-            nc.gpsimd.tensor_tensor(out=wide[:], in0=res[:], in1=ostd_bc[:], op=ALU.mult)
-            parts[i] = (res, wide)
+            parts["res", i] = res
 
-        def finish_b(i):
-            res, wide = parts[i]
+        def new_sums(key):
+            sums = small.tile([P, PAIR], F32, tag="sums")
+            parts[key] = sums
+
+        def square_sum(what, i, sums, col):
             junk = tail.tile([P, D_OUT], BF16)
-            ss1 = small.tile([P, 1], F32)
-            nc.scalar.activation(out=junk[:], in_=res[:], func=ACT.Square, accum_out=ss1[:])
-            over = small.tile([P, 1], F32)
-            nc.scalar.activation(out=over[:], in_=ss1[:], func=ACT.Relu, scale=1.0 / limit_sq, bias=-1.0)
-            clamp = small.tile([P, 1], F32)
-            nc.scalar.activation(out=clamp[:], in_=over[:], func=ACT.Abs_reciprocal_sqrt, bias=1.0)
+            nc.scalar.activation(
+                out=junk[:], in_=parts[what, i][:], func=ACT.Square, accum_out=parts[sums][:, col : col + 1]
+            )
+
+        def clamp_factor(sums, target, lo, hi):
+            if target not in parts:
+                over = small.tile([P, PAIR], F32, tag="over")
+                factor = small.tile([P, PAIR], F32, tag="factor")
+                parts[target, "over"] = over
+                parts[target] = factor
+            nc.scalar.activation(
+                out=parts[target, "over"][:, lo:hi], in_=parts[sums][:, lo:hi], func=ACT.Relu,
+                scale=1.0 / limit_sq, bias=-1.0,
+            )
+            nc.scalar.activation(
+                out=parts[target][:, lo:hi], in_=parts[target, "over"][:, lo:hi], func=ACT.Abs_reciprocal_sqrt, bias=1.0
+            )
+
+        def norm_factor(sums, target, lo, hi):
+            if target not in parts:
+                over = small.tile([P, PAIR], F32, tag="over")
+                factor = small.tile([P, PAIR], F32, tag="factor")
+                parts[target, "over"] = over
+                parts[target] = factor
+            nc.scalar.activation(
+                out=parts[target, "over"][:, lo:hi], in_=parts[sums][:, lo:hi], func=ACT.Relu, bias=-EPS * EPS
+            )
+            nc.scalar.activation(
+                out=parts[target][:, lo:hi], in_=parts[target, "over"][:, lo:hi], func=ACT.Abs_reciprocal_sqrt,
+                bias=EPS * EPS,
+            )
+
+        def times_ostd(i):
+            wide = tail.tile([P, D_OUT], F32)
+            nc.vector.tensor_tensor(out=wide[:], in0=parts["res", i][:], in1=ostd_bc[:], op=ALU.mult)
+            parts["wide", i] = wide
+
+        def clamp_add(i, factor, col):
             mapped = tail.tile([P, D_OUT], F32)
             nc.vector.scalar_tensor_tensor(
-                out=mapped[:], in0=wide[:], scalar=clamp[:], in1=resid[:, i, :], op0=ALU.mult, op1=ALU.add
+                out=mapped[:], in0=parts["wide", i][:], scalar=parts[factor][:, col : col + 1], in1=resid[:, i, :],
+                op0=ALU.mult, op1=ALU.add,
             )
-            parts[i] = mapped
+            parts["mapped", i] = mapped
 
-        def finish_c(i):
-            mapped = parts[i]
-            junk = tail.tile([P, D_OUT], BF16)
-            ss2 = small.tile([P, 1], F32)
-            nc.scalar.activation(out=junk[:], in_=mapped[:], func=ACT.Square, accum_out=ss2[:])
-            over2 = small.tile([P, 1], F32)
-            nc.scalar.activation(out=over2[:], in_=ss2[:], func=ACT.Relu, bias=-EPS * EPS)
-            rnorm = small.tile([P, 1], F32)
-            nc.scalar.activation(out=rnorm[:], in_=over2[:], func=ACT.Abs_reciprocal_sqrt, bias=EPS * EPS)
+        def scale_store(i, factor, col):
             result = tail.tile([P, D_OUT], F32)
-            nc.gpsimd.tensor_scalar(
-                out=result[:], in0=mapped[:], scalar1=rnorm[:], scalar2=0.0, op0=ALU.mult, op1=ALU.add
+            nc.vector.tensor_scalar(
+                out=result[:], in0=parts["mapped", i][:], scalar1=parts[factor][:, col : col + 1], scalar2=None,
+                op0=ALU.mult,
             )
             nc.sync.dma_start(out=out_tiles[i], in_=result[:])
 
-        for i in range(3):
-            normalise_x(i)
-        for i in range(2):
-            quantise_x(i, turn_x(i))
-        layer1(0)
-        for s in range(N_STEPS + 4):
-            i, half = divmod(s, 2)
-            if s + 1 < N_STEPS:
-                layer1(s + 1)
-            if half == 0 and i + 3 < N_TILES:
-                normalise_x(i + 3)
-            xg = None
-            if half == 1 and i + 2 < N_TILES:
-                xg = turn_x(i + 2)
-            if s < N_STEPS:
-                turn_h(s)
-            if xg is not None:
-                quantise_x(i + 2, xg)
-            if s < N_STEPS:
-                quantise_h(s)
-            if 1 <= s <= N_STEPS:
-                layer2(s - 1)
-            if half == 0 and 1 <= i <= N_TILES:
-                finish_a(i - 1)
-            if half == 1 and 1 <= i <= N_TILES:
-                finish_b(i - 1)
-            if half == 0 and 2 <= i <= N_TILES + 1:
-                finish_c(i - 2)
+        extras = {}
+
+        def at(step, fn, *args):
+            extras.setdefault(step, []).append((fn, args))
+
+        def plan_end(j, first, steps, joint):
+            a, b = PAIR * j, PAIR * j + 1
+            s1, s2, c1, c2 = ("s1", j), ("s2", j), ("c1", j), ("c2", j)
+            at(first + steps[0], add_b2, a)
+            at(first + steps[0], new_sums, s1)
+            at(first + steps[0], new_sums, s2)
+            at(first + steps[1], add_b2, b)
+            at(first + steps[1], square_sum, "res", a, s1, 0)
+            if not joint:
+                at(first + steps[1], clamp_factor, s1, c1, 0, 1)
+            at(first + steps[2], times_ostd, a)
+            at(first + steps[2], square_sum, "res", b, s1, 1)
+            if joint:
+                at(first + steps[2], clamp_factor, s1, c1, 0, 2)
+            else:
+                at(first + steps[2], clamp_factor, s1, c1, 1, 2)
+            at(first + steps[3], times_ostd, b)
+            at(first + steps[4], clamp_add, a, c1, 0)
+            at(first + steps[5], clamp_add, b, c1, 1)
+            at(first + steps[5], square_sum, "mapped", a, s2, 0)
+            if not joint:
+                at(first + steps[5], norm_factor, s2, c2, 0, 1)
+            at(first + steps[6], square_sum, "mapped", b, s2, 1)
+            if joint:
+                at(first + steps[6], norm_factor, s2, c2, 0, 2)
+            else:
+                at(first + steps[6], norm_factor, s2, c2, 1, 2)
+            at(first + steps[7], scale_store, a, c2, 0)
+            at(first + steps[8], scale_store, b, c2, 1)
+
+        for g in range(2, N_GROUPS):
+            at(g - 2, permute_w1, g)
+        at(6, spread, sign_col[:, 0:1], shift_bc)
+        at(7, spread, ident_bf[:, 2:3], b2_bc)
+        at(8, spread, ident_bf[:, 3:4], ostd_bc)
+        for j in range(N_PAIRS):
+            at(N_GROUPS * j + 9, make_resid, PAIR * j)
+            at(N_GROUPS * j + 10, make_resid, PAIR * j + 1)
+        for j in (2, 3):
+            first = N_GROUPS * (j - 1)
+            at(first, turn_x, j)
+            at(first + 1, normalise_x, j, (0, 1))
+            at(first + 2, normalise_x, j, (2, 3))
+            at(first + 3, interleave, ("x", j))
+            at(first + 4, quantise_x, j)
+        LAG = 3
+        plan_end(0, N_GROUPS + LAG, (0, 1, 2, 3, 4, 5, 6, 7, 8), True)
+        plan_end(1, 2 * N_GROUPS + LAG, (0, 1, 2, 3, 4, 5, 6, 7, 8), True)
+        plan_end(2, 3 * N_GROUPS + LAG, (0, 0, 1, 1, 2, 2, 3, 4, 4), True)
+        plan_end(3, 4 * N_GROUPS + LAG, (0, 0, 0, 0, 1, 1, 1, 2, 2), False)
+
+        turn_x(0)
+        turn_x(1)
+        normalise_x(0, (0, 1, 2, 3))
+        normalise_x(1, (0, 1, 2, 3))
+        permute_w1(0)
+        interleave(("x", 0))
+        nc.vector.tensor_copy(out=b1_cols[:], in_=b1_raw[:].rearrange("p g t -> p (g t)"))
+        quantise_x(0)
+        permute_w1(1)
+        interleave(("x", 1))
+        layer1_half(0, 0)
+        layer1_half(0, 1)
+        quantise_x(1)
+        last_step = max(extras)
+        for k in range(last_step + 1):
+            if 0 <= k - 1 < N_UNITS:
+                interleave(k - 1)
+            if 0 <= k - 2 < N_UNITS:
+                quantise_h(k - 2)
+            for half in range(2):
+                if k + 1 < N_UNITS:
+                    layer1_half(k + 1, half)
+                if 0 <= k - LAG < N_UNITS:
+                    layer2_tile(k - LAG, half)
+            if k < N_UNITS:
+                bias_relu(k)
+            for fn, args in extras.get(k, []):
+                fn(*args)

@@ -43,27 +43,26 @@ def tile_mlp_kernel(
         acc_pool = ctx.enter_context(tc.psum_pool(name="acc_pool", bufs=4))
 
         x_sb = keep.tile([P, N_TILES, D_IN], BF16)
-        mean4 = keep.tile([P, PACK], BF16)
         std4 = keep.tile([P, PACK], BF16)
         b1_raw = keep.tile([P, N_GROUPS, PACK], BF16)
         vec_rows = keep.tile([P, D_OUT], BF16)
         w1_raw = keep.tile([P, D_HID], I32)
         w1_words = keep.tile([P, N_GROUPS, PACK, P], I32, align_bytes=64)
-        w1s_raw = keep.tile([P, D_HID], U8)
-        w1_planes = keep.tile([P, N_GROUPS, PACK, P], U8, align_bytes=64)
+        w1s_raw = keep.tile([P, 2 * K_PASS], U8)
+        w1_planes = keep.tile([P, 2, PACK, P], U8, align_bytes=64)
         w2_words = keep.tile([P, N_GROUPS, D_OUT * PACK], U8, align_bytes=64)
-        w2_planes = keep.tile([P, N_GROUPS, D_OUT], U8, align_bytes=64)
+        w2_planes = keep.tile([P, 2, D_OUT], U8, align_bytes=64)
         x_words = keep.tile([P, BATCH], U32, align_bytes=64)
         x_planes = keep.tile([P, BATCH], U8, align_bytes=64)
+        b2_bc = keep.tile([P, D_OUT], BF16)
+        ostd_bc = keep.tile([P, D_OUT], BF16)
 
-        nc.vector.memset(w1s_raw[:].bitcast(I32), 0)
         nc.vector.memset(vec_rows[:], 0.0)
+        nc.vector.memset(w1s_raw[:].bitcast(I32), 0)
         nc.vector.memset(w2_planes[:].bitcast(I32), 0)
         warm = keep.tile([P, 1], F32)
         nc.vector.memset(warm[:], 1.0)
         nc.scalar.activation(out=warm[:], in_=warm[:], func=ACT.Abs_reciprocal_sqrt)
-        ident = keep.tile([P, P], F32)
-        make_identity(nc, ident[:])
         ident_bf = keep.tile([P, P], BF16)
         make_identity(nc, ident_bf[:])
 
@@ -83,26 +82,26 @@ def tile_mlp_kernel(
         def load_w2(g):
             nc.sync.dma_start(out=w2_words[:, g : g + 1, :].bitcast(I32), in_=w2_dram[:, g : g + 1, :].bitcast(I32))
 
-        nc.sync.dma_start(out=mean4[:], in_=in_mean.rearrange("(p t) -> p t", t=PACK))
         nc.sync.dma_start(out=std4[:], in_=in_std.rearrange("(p t) -> p t", t=PACK))
         load_x(0)
+        for r, vec in enumerate((out_mean, in_mean)):
+            nc.sync.dma_start(out=vec_rows[r : r + 1, :], in_=vec.rearrange("(o n) -> o n", o=1))
         for q in range(4):
             nc.sync.dma_start(
-                out=w1s_raw[32 * q : 32 * q + 4, :].bitcast(I32),
-                in_=W1_scales[0, 4 * q : 4 * q + 4, :].bitcast(I32),
+                out=w1s_raw[32 * q : 32 * q + 16, :].bitcast(I32),
+                in_=W1_scales[0, 4 * q : 4 * q + 4, :].rearrange("r (j n) -> j r n", j=4).bitcast(I32),
             )
         load_w1(0)
         nc.sync.dma_start(out=b1_raw[:], in_=b1.rearrange("(g p t) -> p g t", p=P, t=PACK))
         load_x(1)
-        for r, vec in enumerate((out_mean, in_mean, b2, out_std)):
-            nc.sync.dma_start(out=vec_rows[r : r + 1, :], in_=vec.rearrange("(o n) -> o n", o=1))
         for g in range(1, 5):
             load_w1(g)
-        for q in range(4):
-            nc.sync.dma_start(
-                out=w2_planes[32 * q : 32 * q + 4, :, :].bitcast(I32),
-                in_=W2_scales[:, 4 * q : 4 * q + 4, :].rearrange("g r n -> r g n").bitcast(I32),
-            )
+        for h in range(2):
+            for q in range(4):
+                nc.sync.dma_start(
+                    out=w2_planes[32 * q : 32 * q + 16, h, :].bitcast(I32),
+                    in_=W2_scales[4 * h : 4 * h + 4, 4 * q : 4 * q + 4, :].bitcast(I32),
+                )
         load_w2(0)
         load_w1(5)
         load_w2(1)
@@ -113,20 +112,20 @@ def tile_mlp_kernel(
             load_w2(g)
         load_x(2)
         load_x(3)
+        nc.sync.dma_start(out=b2_bc[:], in_=b2.partition_broadcast(P))
+        nc.sync.dma_start(out=ostd_bc[:], in_=out_std.partition_broadcast(P))
 
         rstd4 = keep.tile([P, PACK], F32)
         nc.vector.reciprocal(out=rstd4[:], in_=std4[:])
-        shift4 = keep.tile([P, PACK], F32)
-        nc.vector.scalar_tensor_tensor(
-            out=shift4[:], in0=mean4[:], scalar=-1.0, in1=rstd4[:], op0=ALU.mult, op1=ALU.mult
+        minus_col = keep.tile([P, 1], F32)
+        nc.vector.tensor_scalar(out=minus_col[:], in0=ident_bf[:, 1:2], scalar1=-1.0, scalar2=None, op0=ALU.mult)
+        minus_row = keep.tile([P, P], BF16)
+        nc.vector.tensor_scalar(
+            out=minus_row[:], in0=ident_bf[:], scalar1=0.0, scalar2=minus_col[:, 0:1], op0=ALU.mult, op1=ALU.add
         )
         sign_col = keep.tile([P, 1], BF16)
         nc.vector.tensor_tensor(out=sign_col[:], in0=ident_bf[:, 0:1], in1=ident_bf[:, 1:2], op=ALU.subtract)
         b1_cols = keep.tile([P, N_GROUPS * PACK], F32)
-        shift_bc = keep.tile([P, D_OUT], F32)
-        b2_bc = keep.tile([P, D_OUT], F32)
-        ostd_bc = keep.tile([P, D_OUT], F32)
-        resid = keep.tile([P, N_TILES, D_OUT], F32)
 
         banks = {}
         row_tiles = {}
@@ -140,34 +139,35 @@ def tile_mlp_kernel(
                 out=w1_words[:, g, :, :],
                 in_=w1_raw[:, g * K_PASS : (g + 1) * K_PASS].rearrange("p (m t) -> p t m", t=PACK),
             )
+
+        def permute_planes(h):
             nc.vector.tensor_copy(
-                out=w1_planes[:, g, :, :],
-                in_=w1s_raw[:, g * K_PASS : (g + 1) * K_PASS].rearrange("p (m t) -> p t m", t=PACK),
+                out=w1_planes[:, h, :, :],
+                in_=w1s_raw[:, h * K_PASS : (h + 1) * K_PASS].rearrange("p (m t) -> p t m", t=PACK),
             )
 
-        def turn_x(j):
-            xt = hp_pool.tile([P, PAIR, 2, P], F32, tag="hp")
-            for i in range(PAIR):
-                words = x_sb[:, PAIR * j + i, :].bitcast(F32).rearrange("b (p u) -> b u p", u=2)
-                for u in range(2):
-                    nc.tensor.transpose(xt[:, i, u, :], words[:, u, :], ident[:])
-            banks["x", j] = xt
-
-        def normalise_x(j, t_list):
-            if ("x", j) not in row_tiles:
-                x_new = rows.tile([P, PACK, WIDTH], BF16, tag="rows")
-                row_tiles["x", j] = x_new
-            xr = row_tiles["x", j]
-            view = banks["x", j][:].rearrange("p i u b -> p (i u b)").bitcast(BF16)
-            view = view.rearrange("p (i u b e) -> p u e i b", i=PAIR, u=2, e=2)
+        def turn_x(i, t_list):
+            if ("x", i) not in banks:
+                xt_new = hp_pool.tile([P, PACK, P], F32, tag="hp")
+                banks["x", i] = xt_new
+            xt = banks["x", i]
+            x_cols = x_sb[:, i, :].rearrange("b (p t) -> b t p", t=PACK)
+            mean_cols = vec_rows[:].rearrange("k (p t) -> k t p", t=PACK)
             for t in t_list:
-                nc.scalar.activation(
-                    out=xr[:, t, :].rearrange("p (i b) -> p i b", i=PAIR),
-                    in_=view[:, t // 2, t % 2, :, :],
-                    func=ACT.Identity,
-                    scale=rstd4[:, t : t + 1],
-                    bias=shift4[:, t : t + 1],
-                )
+                nc.tensor.matmul(out=xt[:, t, :], lhsT=x_cols[:, t, :], rhs=ident_bf[:], start=True, stop=False)
+                nc.tensor.matmul(out=xt[:, t, :], lhsT=mean_cols[:, t, :], rhs=minus_row[:], start=False, stop=True)
+
+        def normalise_x(i):
+            j, half = divmod(i, PAIR)
+            if ("x", j) not in grouped_tiles:
+                x_new = grouped.tile([P, WIDTH * PACK], BF16, align_bytes=64, tag="grouped")
+                grouped_tiles["x", j] = x_new
+            nc.vector.tensor_tensor(
+                out=grouped_tiles["x", j][:, half * K_PASS : (half + 1) * K_PASS].rearrange("p (b t) -> p b t", t=PACK),
+                in0=banks["x", i][:].rearrange("p t b -> p b t"),
+                in1=rstd4[:].unsqueeze(1).to_broadcast([P, P, PACK]),
+                op=ALU.mult,
+            )
 
         def interleave(key):
             g_new = grouped.tile([P, WIDTH * PACK], BF16, align_bytes=64, tag="grouped")
@@ -191,7 +191,7 @@ def tile_mlp_kernel(
                 nc.tensor.matmul_mx(
                     out=hp[:, e, :],
                     lhsT=w1_words[:, g, t, :].bitcast(FP8X4),
-                    lhsT_scale=w1_planes[:, g, t, :],
+                    lhsT_scale=w1_planes[4 * (g // 2) : P, g % 2, t, :],
                     rhs=x_words[:, cols].bitcast(FP8X4),
                     rhs_scale=x_planes[:, cols],
                     start=True,
@@ -228,18 +228,18 @@ def tile_mlp_kernel(
                 lhsT=hq[:, i * P : (i + 1) * P].bitcast(FP8X4),
                 lhsT_scale=hsc[:, i * P : (i + 1) * P],
                 rhs=w2_words[:, g, :].bitcast(FP8X4),
-                rhs_scale=w2_planes[:, g, :],
+                rhs_scale=w2_planes[4 * (g % 4) : P, g // 4, :],
                 start=(g == 0),
                 stop=(g == N_GROUPS - 1),
             )
 
-        def spread(column, target):
-            ps = hp_pool.tile([P, D_OUT], F32, tag="hp")
-            nc.tensor.matmul(out=ps[:], lhsT=column.to_broadcast([P, P]), rhs=vec_rows[:], start=True, stop=True)
-            nc.scalar.copy(out=target[:], in_=ps[:])
-
         def make_resid(i):
-            nc.vector.tensor_tensor(out=resid[:, i, :], in0=x_sb[:, i, :], in1=shift_bc[:], op=ALU.add)
+            rp = hp_pool.tile([P, D_OUT], F32, tag="hp")
+            nc.tensor.matmul(out=rp[:], lhsT=ident_bf[:], rhs=x_sb[:, i, :], start=True, stop=False)
+            nc.tensor.matmul(
+                out=rp[:], lhsT=sign_col[:, 0:1].to_broadcast([P, P]), rhs=vec_rows[:], start=False, stop=True
+            )
+            parts["resid", i] = rp
 
         limit_sq = float(norm_max) * float(norm_max)
         out_tiles = out.rearrange("(n p) o -> n p o", p=P)
@@ -295,7 +295,8 @@ def tile_mlp_kernel(
         def clamp_add(i, factor, col):
             mapped = tail.tile([P, D_OUT], F32)
             nc.vector.scalar_tensor_tensor(
-                out=mapped[:], in0=parts["wide", i][:], scalar=parts[factor][:, col : col + 1], in1=resid[:, i, :],
+                out=mapped[:], in0=parts["wide", i][:], scalar=parts[factor][:, col : col + 1],
+                in1=parts["resid", i][:],
                 op0=ALU.mult, op1=ALU.add,
             )
             parts["mapped", i] = mapped
@@ -330,7 +331,9 @@ def tile_mlp_kernel(
             else:
                 at(first + steps[2], clamp_factor, s1, c1, 1, 2)
             at(first + steps[3], times_ostd, b)
+            at(first + max(steps[4] - 1, 0), make_resid, a)
             at(first + steps[4], clamp_add, a, c1, 0)
+            at(first + max(steps[5] - 1, 0), make_resid, b)
             at(first + steps[5], clamp_add, b, c1, 1)
             at(first + steps[5], square_sum, "mapped", a, s2, 0)
             if not joint:
@@ -345,44 +348,43 @@ def tile_mlp_kernel(
 
         for g in range(2, N_GROUPS):
             at(g - 2, permute_w1, g)
-        at(6, spread, sign_col[:, 0:1], shift_bc)
-        at(7, spread, ident_bf[:, 2:3], b2_bc)
-        at(8, spread, ident_bf[:, 3:4], ostd_bc)
-        for j in range(N_PAIRS):
-            at(N_GROUPS * j + 9, make_resid, PAIR * j)
-            at(N_GROUPS * j + 10, make_resid, PAIR * j + 1)
-        for j in (2, 3):
+        for j in range(1, N_PAIRS):
             first = N_GROUPS * (j - 1)
-            at(first, turn_x, j)
-            at(first + 1, normalise_x, j, (0, 1))
-            at(first + 2, normalise_x, j, (2, 3))
-            at(first + 3, interleave, ("x", j))
-            at(first + 4, quantise_x, j)
+            at(first, turn_x, PAIR * j, (0, 1))
+            at(first + 1, turn_x, PAIR * j, (2, 3))
+            at(first + 2, normalise_x, PAIR * j)
+            at(first + 2, turn_x, PAIR * j + 1, (0, 1))
+            at(first + 3, turn_x, PAIR * j + 1, (2, 3))
+            at(first + 4, normalise_x, PAIR * j + 1)
+            at(first + 5, quantise_x, j)
         LAG = 3
         plan_end(0, N_GROUPS + LAG, (0, 1, 2, 3, 4, 5, 6, 7, 8), True)
         plan_end(1, 2 * N_GROUPS + LAG, (0, 1, 2, 3, 4, 5, 6, 7, 8), True)
         plan_end(2, 3 * N_GROUPS + LAG, (0, 0, 1, 1, 2, 2, 3, 4, 4), True)
         plan_end(3, 4 * N_GROUPS + LAG, (0, 0, 0, 0, 1, 1, 1, 2, 2), False)
 
-        turn_x(0)
-        turn_x(1)
-        normalise_x(0, (0, 1, 2, 3))
-        normalise_x(1, (0, 1, 2, 3))
+        turn_x(0, (0, 1, 2, 3))
+        turn_x(1, (0, 1, 2, 3))
+        normalise_x(0)
+        permute_planes(0)
         permute_w1(0)
-        interleave(("x", 0))
+        normalise_x(1)
         nc.vector.tensor_copy(out=b1_cols[:], in_=b1_raw[:].rearrange("p g t -> p (g t)"))
         quantise_x(0)
-        permute_w1(1)
-        interleave(("x", 1))
         layer1_half(0, 0)
         layer1_half(0, 1)
-        quantise_x(1)
+        permute_planes(1)
+        permute_w1(1)
         last_step = max(extras)
         for k in range(last_step + 1):
-            if 0 <= k - 1 < N_UNITS:
-                interleave(k - 1)
-            if 0 <= k - 2 < N_UNITS:
+            if k == N_UNITS:
                 quantise_h(k - 2)
+                interleave(k - 1)
+            else:
+                if 0 <= k - 1 < N_UNITS:
+                    interleave(k - 1)
+                if 0 <= k - 2 < N_UNITS:
+                    quantise_h(k - 2)
             for half in range(2):
                 if k + 1 < N_UNITS:
                     layer1_half(k + 1, half)

@@ -172,7 +172,8 @@ def tile_mlp_kernel(
         def interleave(key):
             g_new = grouped.tile([P, WIDTH * PACK], BF16, align_bytes=64, tag="grouped")
             nc.vector.tensor_copy(
-                out=g_new[:].rearrange("p (c t) -> p c t", t=PACK), in_=row_tiles[key][:].rearrange("p t c -> p c t")
+                out=g_new[:].rearrange("p (c i t) -> p c t i", i=4, t=PACK),
+                in_=row_tiles[key][:].rearrange("p t (c i) -> p c t i", i=4),
             )
             grouped_tiles[key] = g_new
 

@@ -359,10 +359,10 @@ def tile_mlp_kernel(
             at(first + 4, normalise_x, PAIR * j + 1)
             at(first + 5, quantise_x, j)
         LAG = 3
-        plan_end(0, N_GROUPS + LAG, (0, 1, 2, 3, 4, 5, 6, 7, 8), True)
-        plan_end(1, 2 * N_GROUPS + LAG, (0, 1, 2, 3, 4, 5, 6, 7, 8), True)
-        plan_end(2, 3 * N_GROUPS + LAG, (0, 0, 1, 1, 2, 2, 3, 4, 4), True)
-        plan_end(3, 4 * N_GROUPS + LAG, (0, 0, 0, 0, 1, 1, 1, 2, 2), False)
+        plan_end(0, N_GROUPS + LAG - 1, (0, 1, 2, 3, 4, 5, 6, 7, 8), True)
+        plan_end(1, 2 * N_GROUPS + LAG - 1, (0, 1, 2, 3, 4, 5, 6, 7, 8), True)
+        plan_end(2, 3 * N_GROUPS + LAG - 1, (0, 1, 2, 3, 4, 5, 6, 7, 8), True)
+        plan_end(3, 4 * N_GROUPS + LAG - 1, (0, 0, 0, 0, 1, 1, 1, 2, 2), False)
 
         turn_x(0, (0, 1, 2, 3))
         turn_x(1, (0, 1, 2, 3))

@@ -34,9 +34,9 @@ def tile_mlp_kernel(
     with ExitStack() as ctx:
         ctx.enter_context(tc.manual_schedule())
         keep = ctx.enter_context(tc.tile_pool(name="keep", bufs=1))
-        rows = ctx.enter_context(tc.tile_pool(name="rows", bufs=3))
-        grouped = ctx.enter_context(tc.tile_pool(name="grouped", bufs=3))
-        codes = ctx.enter_context(tc.tile_pool(name="codes", bufs=4))
+        rows = ctx.enter_context(tc.tile_pool(name="rows", bufs=5))
+        grouped = ctx.enter_context(tc.tile_pool(name="grouped", bufs=5))
+        codes = ctx.enter_context(tc.tile_pool(name="codes", bufs=6))
         tail = ctx.enter_context(tc.tile_pool(name="tail", bufs=4))
         small = ctx.enter_context(tc.tile_pool(name="small", bufs=4))
         hp_pool = ctx.enter_context(tc.psum_pool(name="hp_pool", bufs=4))

from contextlib import ExitStack

import concourse.mybir as mybir
from concourse.masks import make_identity

F32 = mybir.dt.float32
BF16 = mybir.dt.bfloat16
I32 = mybir.dt.int32
U32 = mybir.dt.uint32
U8 = mybir.dt.uint8
FP8X4 = mybir.dt.float8_e4m3fn_x4
ALU = mybir.AluOpType
ACT = mybir.ActivationFunctionType

P = 128
PACK = 4
K_PASS = P * PACK
BATCH, D_IN, D_HID, D_OUT = 1024, 512, 4096, 512
N_TILES = BATCH // P
N_GROUPS = D_HID // K_PASS
PAIR = 2
WIDTH = PAIR * P
N_PAIRS = N_TILES // PAIR
N_UNITS = N_PAIRS * N_GROUPS
EPS = 1e-12

FLOPS = 2 * BATCH * D_IN * D_HID + 2 * BATCH * D_HID * D_OUT


def tile_mlp_kernel(
    tc, x, in_mean, in_std, out_mean, out_std, W1_words, W1_scales, b1, W2_words, W2_scales, b2, norm_max, out
):
    nc = tc.nc
    with ExitStack() as ctx:
        ctx.enter_context(tc.manual_schedule())
        keep = ctx.enter_context(tc.tile_pool(name="keep", bufs=1))
        rows = ctx.enter_context(tc.tile_pool(name="rows", bufs=5))
        grouped = ctx.enter_context(tc.tile_pool(name="grouped", bufs=5))
        codes = ctx.enter_context(tc.tile_pool(name="codes", bufs=6))
        tail = ctx.enter_context(tc.tile_pool(name="tail", bufs=4))
        small = ctx.enter_context(tc.tile_pool(name="small", bufs=4))
        hp_pool = ctx.enter_context(tc.psum_pool(name="hp_pool", bufs=4))
        acc_pool = ctx.enter_context(tc.psum_pool(name="acc_pool", bufs=4))

        x_sb = keep.tile([P, N_TILES, D_IN], BF16)
        std4 = keep.tile([P, PACK], BF16)
        b1_raw = keep.tile([P, N_GROUPS, PACK], BF16)
        vec_rows = keep.tile([P, D_OUT], BF16)
        w1_raw = keep.tile([P, D_HID], I32)
        w1_words = keep.tile([P, N_GROUPS, PACK, P], I32, align_bytes=64)
        w1s_raw = keep.tile([P, 2 * K_PASS], U8)
        w1_planes = keep.tile([P, 2, PACK, P], U8, align_bytes=64)
        w2_words = keep.tile([P, N_GROUPS, D_OUT * PACK], U8, align_bytes=64)
        w2_planes = keep.tile([P, 2, D_OUT], U8, align_bytes=64)
        x_words = keep.tile([P, BATCH], U32, align_bytes=64)
        x_planes = keep.tile([P, BATCH], U8, align_bytes=64)
        b2_bc = keep.tile([P, D_OUT], BF16)
        ostd_bc = keep.tile([P, D_OUT], BF16)

        nc.vector.memset(vec_rows[:], 0.0)
        nc.vector.memset(w1s_raw[:].bitcast(I32), 0)
        nc.vector.memset(w2_planes[:].bitcast(I32), 0)
        warm = keep.tile([P, 1], F32)
        nc.vector.memset(warm[:], 1.0)
        nc.scalar.activation(out=warm[:], in_=warm[:], func=ACT.Abs_reciprocal_sqrt)
        ident_bf = keep.tile([P, P], BF16)
        make_identity(nc, ident_bf[:])

        x_rows = x.rearrange("(n p) k -> p n k", p=P)
        w1_dram = W1_words[0].rearrange("p n t -> p (n t)")
        w2_dram = W2_words.rearrange("g p n t -> p g (n t)")
        chunk = K_PASS * PACK

        def load_x(j):
            nc.sync.dma_start(out=x_sb[:, PAIR * j : PAIR * (j + 1), :], in_=x_rows[:, PAIR * j : PAIR * (j + 1), :])

        def load_w1(g):
            nc.sync.dma_start(
                out=w1_raw[:, g * K_PASS : (g + 1) * K_PASS], in_=w1_dram[:, g * chunk : (g + 1) * chunk].bitcast(I32)
            )

        def load_w2(g):
            nc.sync.dma_start(out=w2_words[:, g : g + 1, :].bitcast(I32), in_=w2_dram[:, g : g + 1, :].bitcast(I32))

        nc.sync.dma_start(out=std4[:], in_=in_std.rearrange("(p t) -> p t", t=PACK))
        load_x(0)
        for r, vec in enumerate((out_mean, in_mean)):
            nc.sync.dma_start(out=vec_rows[r : r + 1, :], in_=vec.rearrange("(o n) -> o n", o=1))
        for q in range(4):
            nc.sync.dma_start(
                out=w1s_raw[32 * q : 32 * q + 16, :].bitcast(I32),
                in_=W1_scales[0, 4 * q : 4 * q + 4, :].rearrange("r (j n) -> j r n", j=4).bitcast(I32),
            )
        load_w1(0)
        nc.sync.dma_start(out=b1_raw[:], in_=b1.rearrange("(g p t) -> p g t", p=P, t=PACK))
        load_x(1)
        for g in range(1, 5):
            load_w1(g)
        for h in range(2):
            for q in range(4):
                nc.sync.dma_start(
                    out=w2_planes[32 * q : 32 * q + 16, h, :].bitcast(I32),
                    in_=W2_scales[4 * h : 4 * h + 4, 4 * q : 4 * q + 4, :].bitcast(I32),
                )
        load_w2(0)
        load_w1(5)
        load_w2(1)
        load_w1(6)
        load_w2(2)
        load_w1(7)
        for g in range(3, N_GROUPS):
            load_w2(g)
        load_x(2)
        load_x(3)
        nc.sync.dma_start(out=b2_bc[:], in_=b2.partition_broadcast(P))
        nc.sync.dma_start(out=ostd_bc[:], in_=out_std.partition_broadcast(P))

        rstd4 = keep.tile([P, PACK], F32)
        nc.vector.reciprocal(out=rstd4[:], in_=std4[:])
        minus_col = keep.tile([P, 1], F32)
        nc.vector.tensor_scalar(out=minus_col[:], in0=ident_bf[:, 1:2], scalar1=-1.0, scalar2=None, op0=ALU.mult)
        minus_row = keep.tile([P, P], BF16)
        nc.vector.tensor_scalar(
            out=minus_row[:], in0=ident_bf[:], scalar1=0.0, scalar2=minus_col[:, 0:1], op0=ALU.mult, op1=ALU.add
        )
        sign_col = keep.tile([P, 1], BF16)
        nc.vector.tensor_tensor(out=sign_col[:], in0=ident_bf[:, 0:1], in1=ident_bf[:, 1:2], op=ALU.subtract)
        b1_cols = keep.tile([P, N_GROUPS * PACK], F32)

        banks = {}
        row_tiles = {}
        grouped_tiles = {}
        h_codes = {}
        accs = {}
        parts = {}

        def permute_w1(g):
            nc.vector.tensor_copy(
                out=w1_words[:, g, :, :],
                in_=w1_raw[:, g * K_PASS : (g + 1) * K_PASS].rearrange("p (m t) -> p t m", t=PACK),
            )

        def permute_planes(h):
            nc.vector.tensor_copy(
                out=w1_planes[:, h, :, :],
                in_=w1s_raw[:, h * K_PASS : (h + 1) * K_PASS].rearrange("p (m t) -> p t m", t=PACK),
            )

        def turn_x(i, t_list):
            if ("x", i) not in banks:
                xt_new = hp_pool.tile([P, PACK, P], F32, tag="hp")
                banks["x", i] = xt_new
            xt = banks["x", i]
            x_cols = x_sb[:, i, :].rearrange("b (p t) -> b t p", t=PACK)
            mean_cols = vec_rows[:].rearrange("k (p t) -> k t p", t=PACK)
            for t in t_list:
                nc.tensor.matmul(out=xt[:, t, :], lhsT=x_cols[:, t, :], rhs=ident_bf[:], start=True, stop=False)
                nc.tensor.matmul(out=xt[:, t, :], lhsT=mean_cols[:, t, :], rhs=minus_row[:], start=False, stop=True)

        def normalise_x(i):
            j, half = divmod(i, PAIR)
            if ("x", j) not in grouped_tiles:
                x_new = grouped.tile([P, WIDTH * PACK], BF16, align_bytes=64, tag="grouped")
                grouped_tiles["x", j] = x_new
            nc.vector.tensor_tensor(
                out=grouped_tiles["x", j][:, half * K_PASS : (half + 1) * K_PASS].rearrange("p (b t) -> p b t", t=PACK),
                in0=banks["x", i][:].rearrange("p t b -> p b t"),
                in1=rstd4[:].unsqueeze(1).to_broadcast([P, P, PACK]),
                op=ALU.mult,
            )

        def interleave(key):
            g_new = grouped.tile([P, WIDTH * PACK], BF16, align_bytes=64, tag="grouped")
            nc.vector.tensor_copy(
                out=g_new[:].rearrange("p (c i t) -> p c t i", i=4, t=PACK),
                in_=row_tiles[key][:].rearrange("p t (c i) -> p c t i", i=4),
            )
            grouped_tiles[key] = g_new

        def quantise_x(j):
            cols = slice(j * WIDTH, (j + 1) * WIDTH)
            nc.vector.quantize_mx(
                out=x_words[:, cols].bitcast(FP8X4), scales=x_planes[:, cols], in_=grouped_tiles["x", j][:]
            )

        def layer1_half(s, half):
            j, g = divmod(s, N_GROUPS)
            cols = slice(j * WIDTH, (j + 1) * WIDTH)
            hp = hp_pool.tile([P, 2, WIDTH], F32, tag="hp")
            for e in range(2):
                t = 2 * half + e
                nc.tensor.matmul_mx(
                    out=hp[:, e, :],
                    lhsT=w1_words[:, g, t, :].bitcast(FP8X4),
                    lhsT_scale=w1_planes[4 * (g // 2) : P, g % 2, t, :],
                    rhs=x_words[:, cols].bitcast(FP8X4),
                    rhs_scale=x_planes[:, cols],
                    start=True,
                    stop=True,
                )
            banks[s, half] = hp

        def bias_relu(s):
            g = s % N_GROUPS
            hr = rows.tile([P, PACK, WIDTH], BF16, tag="rows")
            for t in range(PACK):
                nc.scalar.activation(
                    out=hr[:, t, :],
                    in_=banks[s, t // 2][:, t % 2, :],
                    func=ACT.Relu,
                    bias=b1_cols[:, PACK * g + t : PACK * g + t + 1],
                )
            row_tiles[s] = hr

        def quantise_h(s):
            hq = codes.tile([P, WIDTH], U32, align_bytes=64)
            hsc = codes.tile([P, WIDTH], U8, align_bytes=64)
            nc.vector.quantize_mx(out=hq[:].bitcast(FP8X4), scales=hsc[:], in_=grouped_tiles[s][:])
            h_codes[s] = (hq, hsc)

        def layer2_tile(s, i):
            j, g = divmod(s, N_GROUPS)
            if g == 0:
                acc_new = acc_pool.tile([P, D_OUT], F32, name="acc")
                accs[PAIR * j + i] = acc_new
            hq, hsc = h_codes[s]
            nc.tensor.matmul_mx(
                out=accs[PAIR * j + i][:],
                lhsT=hq[:, i * P : (i + 1) * P].bitcast(FP8X4),
                lhsT_scale=hsc[:, i * P : (i + 1) * P],
                rhs=w2_words[:, g, :].bitcast(FP8X4),
                rhs_scale=w2_planes[4 * (g % 4) : P, g // 4, :],
                start=(g == 0),
                stop=(g == N_GROUPS - 1),
            )

        def make_resid(i):
            rp = hp_pool.tile([P, D_OUT], F32, tag="hp")
            nc.tensor.matmul(out=rp[:], lhsT=ident_bf[:], rhs=x_sb[:, i, :], start=True, stop=False)
            nc.tensor.matmul(
                out=rp[:], lhsT=sign_col[:, 0:1].to_broadcast([P, P]), rhs=vec_rows[:], start=False, stop=True
            )
            parts["resid", i] = rp

        limit_sq = float(norm_max) * float(norm_max)
        out_tiles = out.rearrange("(n p) o -> n p o", p=P)

        def add_b2(i):
            res = tail.tile([P, D_OUT], F32)
            nc.vector.tensor_tensor(out=res[:], in0=accs[i][:], in1=b2_bc[:], op=ALU.add)
            parts["res", i] = res

        def new_sums(key):
            sums = small.tile([P, PAIR], F32, tag="sums")
            parts[key] = sums

        def square_sum(what, i, sums, col):
            junk = tail.tile([P, D_OUT], BF16)
            nc.scalar.activation(
                out=junk[:], in_=parts[what, i][:], func=ACT.Square, accum_out=parts[sums][:, col : col + 1]
            )

        def clamp_factor(sums, target, lo, hi):
            if target not in parts:
                over = small.tile([P, PAIR], F32, tag="over")
                factor = small.tile([P, PAIR], F32, tag="factor")
                parts[target, "over"] = over
                parts[target] = factor
            nc.scalar.activation(
                out=parts[target, "over"][:, lo:hi], in_=parts[sums][:, lo:hi], func=ACT.Relu,
                scale=1.0 / limit_sq, bias=-1.0,
            )
            nc.scalar.activation(
                out=parts[target][:, lo:hi], in_=parts[target, "over"][:, lo:hi], func=ACT.Abs_reciprocal_sqrt, bias=1.0
            )

        def norm_factor(sums, target, lo, hi):
            if target not in parts:
                over = small.tile([P, PAIR], F32, tag="over")
                factor = small.tile([P, PAIR], F32, tag="factor")
                parts[target, "over"] = over
                parts[target] = factor
            nc.scalar.activation(
                out=parts[target, "over"][:, lo:hi], in_=parts[sums][:, lo:hi], func=ACT.Relu, bias=-EPS * EPS
            )
            nc.scalar.activation(
                out=parts[target][:, lo:hi], in_=parts[target, "over"][:, lo:hi], func=ACT.Abs_reciprocal_sqrt,
                bias=EPS * EPS,
            )

        def times_ostd(i):
            wide = tail.tile([P, D_OUT], F32)
            nc.vector.tensor_tensor(out=wide[:], in0=parts["res", i][:], in1=ostd_bc[:], op=ALU.mult)
            parts["wide", i] = wide

        def clamp_add(i, factor, col):
            mapped = tail.tile([P, D_OUT], F32)
            nc.vector.scalar_tensor_tensor(
                out=mapped[:], in0=parts["wide", i][:], scalar=parts[factor][:, col : col + 1],
                in1=parts["resid", i][:],
                op0=ALU.mult, op1=ALU.add,
            )
            parts["mapped", i] = mapped

        def scale_store(i, factor, col):
            result = tail.tile([P, D_OUT], F32)
            nc.vector.tensor_scalar(
                out=result[:], in0=parts["mapped", i][:], scalar1=parts[factor][:, col : col + 1], scalar2=None,
                op0=ALU.mult,
            )
            nc.sync.dma_start(out=out_tiles[i], in_=result[:])

        extras = {}

        def at(step, fn, *args):
            extras.setdefault(step, []).append((fn, args))

        def plan_end(j, first, steps, joint):
            a, b = PAIR * j, PAIR * j + 1
            s1, s2, c1, c2 = ("s1", j), ("s2", j), ("c1", j), ("c2", j)
            at(first + steps[0], add_b2, a)
            at(first + steps[0], new_sums, s1)
            at(first + steps[0], new_sums, s2)
            at(first + steps[1], add_b2, b)
            at(first + steps[1], square_sum, "res", a, s1, 0)
            if not joint:
                at(first + steps[1], clamp_factor, s1, c1, 0, 1)
            at(first + steps[2], times_ostd, a)
            at(first + steps[2], square_sum, "res", b, s1, 1)
            if joint:
                at(first + steps[2], clamp_factor, s1, c1, 0, 2)
            else:
                at(first + steps[2], clamp_factor, s1, c1, 1, 2)
            at(first + steps[3], times_ostd, b)
            at(first + max(steps[4] - 1, 0), make_resid, a)
            at(first + steps[4], clamp_add, a, c1, 0)
            at(first + max(steps[5] - 1, 0), make_resid, b)
            at(first + steps[5], clamp_add, b, c1, 1)
            at(first + steps[5], square_sum, "mapped", a, s2, 0)
            if not joint:
                at(first + steps[5], norm_factor, s2, c2, 0, 1)
            at(first + steps[6], square_sum, "mapped", b, s2, 1)
            if joint:
                at(first + steps[6], norm_factor, s2, c2, 0, 2)
            else:
                at(first + steps[6], norm_factor, s2, c2, 1, 2)
            at(first + steps[7], scale_store, a, c2, 0)
            at(first + steps[8], scale_store, b, c2, 1)

        for g in range(2, N_GROUPS):
            at(g - 2, permute_w1, g)
        for j in range(1, N_PAIRS):
            first = N_GROUPS * (j - 1)
            at(first, turn_x, PAIR * j, (0, 1))
            at(first + 1, turn_x, PAIR * j, (2, 3))
            at(first + 2, normalise_x, PAIR * j)
            at(first + 2, turn_x, PAIR * j + 1, (0, 1))
            at(first + 3, turn_x, PAIR * j + 1, (2, 3))
            at(first + 4, normalise_x, PAIR * j + 1)
            at(first + 5, quantise_x, j)
        LAG = 3
        plan_end(0, N_GROUPS + LAG - 1, (0, 1, 2, 3, 4, 5, 6, 7, 8), True)
        plan_end(1, 2 * N_GROUPS + LAG - 1, (0, 1, 2, 3, 4, 5, 6, 7, 8), True)
        plan_end(2, 3 * N_GROUPS + LAG - 1, (0, 1, 2, 3, 4, 5, 6, 7, 8), True)
        plan_end(3, 4 * N_GROUPS + LAG - 1, (0, 0, 0, 0, 1, 1, 1, 2, 2), False)

        turn_x(0, (0, 1, 2, 3))
        turn_x(1, (0, 1, 2, 3))
        normalise_x(0)
        permute_planes(0)
        permute_w1(0)
        normalise_x(1)
        nc.vector.tensor_copy(out=b1_cols[:], in_=b1_raw[:].rearrange("p g t -> p (g t)"))
        quantise_x(0)
        layer1_half(0, 0)
        layer1_half(0, 1)
        permute_planes(1)
        permute_w1(1)
        last_step = max(extras)
        for k in range(last_step + 1):
            if k == N_UNITS:
                quantise_h(k - 2)
                interleave(k - 1)
            else:
                if 0 <= k - 1 < N_UNITS:
                    interleave(k - 1)
                if 0 <= k - 2 < N_UNITS:
                    quantise_h(k - 2)
            for half in range(2):
                if k + 1 < N_UNITS:
                    layer1_half(k + 1, half)
                if 0 <= k - LAG < N_UNITS:
                    layer2_tile(k - LAG, half)
            if k < N_UNITS:
                bias_relu(k)
            for fn, args in extras.get(k, []):
                fn(*args)
